import numpy as np
import ml_dtypes


def mxq(x, axis, fmt="e4m3"):
    dtype, down = {"e4m3": (ml_dtypes.float8_e4m3fn, 7), "e5m2": (ml_dtypes.float8_e5m2, 14)}[fmt]
    v = np.moveaxis(np.asarray(x, np.float32).astype(ml_dtypes.bfloat16).astype(np.float64), axis, -1)
    blocks = v.reshape(v.shape[:-1] + (-1, 32))
    amax = np.abs(blocks).max(-1, keepdims=True)
    byte = np.maximum(np.where(amax > 0, np.frexp(amax)[1] - 1 + 127, 0) - down, 1)
    scale = np.exp2(byte - 127.0)
    codes = (blocks / scale).astype(np.float32).astype(dtype).astype(np.float64)
    return np.moveaxis((codes * scale).reshape(v.shape), -1, axis)


WIDE = False


def mx_kscale(k):
    if not WIDE:
        return np.ones(k)
    levels = np.array([10, -10, 5, -5, 0])
    a = np.random.permutation(np.resize(levels, k // 512 * 4)).reshape(k // 512, 4)
    idx = np.arange(k)
    return np.exp2(a[idx // 512, idx % 128 // 32])


BF16 = ml_dtypes.bfloat16


def bf(x):
    return np.asarray(x, np.float32).astype(BF16)


def f64(x):
    return np.asarray(x).astype(np.float64)


BATCH, SEQ, IN_DIM, MID_DIM, OUT_DIM = 4, 2048, 512, 512, 512
CB = 2.0 ** -np.round(np.log2(IN_DIM) / 2)
CA = 2.0 ** -np.round(np.log2(MID_DIM) / 2)


def signs(shape):
    return np.where(np.random.standard_normal(shape) >= 0, 1.0, -1.0)


def setup_inputs():
    s, t = mx_kscale(IN_DIM), mx_kscale(MID_DIM)
    return {"x": bf(np.random.standard_normal((BATCH, SEQ, IN_DIM)) * s),
            "scaling0": bf(0.5 + np.random.uniform(size=IN_DIM)),
            "B": bf(signs((MID_DIM, IN_DIM)) * CB / s[None, :]),
            "scaling2": bf((0.5 + np.random.uniform(size=MID_DIM)) * t),
            "A": bf(signs((OUT_DIM, MID_DIM)) * CA / t[None, :]),
            "scaling4": bf(0.5 + np.random.uniform(size=OUT_DIM)),
            "bias": bf(np.random.standard_normal(OUT_DIM))}


def reference(x, scaling0, B, scaling2, A, scaling4, bias):
    h = f64(x) * f64(scaling0)
    h = mxq(h, 2, "e4m3") @ mxq(f64(B), 1, "e4m3").T
    h = h * f64(scaling2)
    h = mxq(h, 2, "e4m3") @ mxq(f64(A), 1, "e4m3").T
    return h * f64(scaling4) + f64(bias)

@@ -1,0 +1,196 @@
+from contextlib import ExitStack
+
+import concourse.mybir as mybir
+from concourse.masks import make_identity
+
+F32 = mybir.dt.float32
+BF16 = mybir.dt.bfloat16
+U32 = mybir.dt.uint32
+U8 = mybir.dt.uint8
+FP8X4 = mybir.dt.float8_e4m3fn_x4
+ACT = mybir.ActivationFunctionType
+ALU = mybir.AluOpType
+
+P = 128
+DIM = 512
+TOKENS = 4 * 2048
+ROUND = 512
+ROUNDS = TOKENS // ROUND
+FLOPS = 2 * 2 * TOKENS * DIM * DIM
+
+
+def tile_doublebinarylinear_t_kernel(tc, x, scaling0, B, scaling2, A, scaling4, bias, out):
+    nc = tc.nc
+    x_rounds = x.flatten_outer_dims().rearrange("(r p i) k -> r p i k", p=P, i=4)
+    out_rounds = out.flatten_outer_dims().rearrange("(r p i) o -> r p i o", p=P, i=4)
+
+    with ExitStack() as ctx:
+        ctx.enter_context(tc.manual_schedule())
+        keep = ctx.enter_context(tc.tile_pool(name="keep", bufs=1))
+        work = ctx.enter_context(tc.tile_pool(name="work", bufs=2))
+        psum = ctx.enter_context(tc.psum_pool(name="psum", bufs=1))
+
+        s0_t = keep.tile([P, 2, 2], BF16, name="s0_t")
+        s2_t = keep.tile([P, 4], BF16, name="s2_t")
+        s4_b = keep.tile([P, 4], BF16, name="s4_b")
+        bias_b = keep.tile([P, 4], BF16, name="bias_b")
+        nc.scalar.dma_start(out=s0_t[:], in_=scaling0.rearrange("(u p e) -> p u e", u=2, e=2))
+        nc.scalar.dma_start(out=s2_t[:], in_=scaling2.rearrange("(q j) -> q j", j=4))
+        with nc.allow_non_contiguous_dma(reason="two vectors of 512 values, one value a partition and chunk"):
+            nc.scalar.dma_start(out=s4_b[:], in_=scaling4.rearrange("(c r) -> r c", c=4))
+            nc.scalar.dma_start(out=bias_b[:], in_=bias.rearrange("(c r) -> r c", c=4))
+
+        b_sb = keep.tile([P, 4, DIM], BF16, name="b_sb")
+        a_sb = keep.tile([P, 4, DIM], BF16, name="a_sb")
+        x_sb = [keep.tile([P, 4, DIM], BF16, name="x_sb%d" % r) for r in range(ROUNDS)]
+        nc.sync.dma_start(out=b_sb[:], in_=B.rearrange("(q j) k -> q j k", j=4))
+        nc.sync.dma_start(out=x_sb[0][:], in_=x_rounds[0])
+        nc.sync.dma_start(out=x_sb[1][:], in_=x_rounds[1])
+        nc.sync.dma_start(out=a_sb[:], in_=A.rearrange("(c r) m -> r c m", c=4))
+        for r in range(2, ROUNDS):
+            nc.sync.dma_start(out=x_sb[r][:], in_=x_rounds[r])
+
+        ident = keep.tile([P, P], F32, name="ident")
+        make_identity(nc, ident[:])
+        s4_t = keep.tile([P, 4], F32, name="s4_t")
+        bias_t = keep.tile([P, 4], F32, name="bias_t")
+
+        banks_made = []
+
+        def new_bank():
+            n = len(banks_made) % 8
+            banks_made.append(n)
+            return psum.tile([P, 512], F32, name="bank%d" % n, tag="bank%d" % n)
+
+        def transpose_half(src, half, stepped):
+            bank = new_bank()
+            for u in range(2):
+                for il in range(2):
+                    words = src[:, 2 * half + il, :].bitcast(F32)
+                    if stepped:
+                        block = words.rearrange("p (q u) -> p u q", u=2)[:, u, :]
+                    else:
+                        block = words[:, u * P : (u + 1) * P]
+                    col = (2 * u + il) * P
+                    nc.tensor.transpose(bank[:, col : col + P], block, ident[:])
+            return bank
+
+        def prepare_weight(src, stepped, label):
+            grouped = keep.tile([P, 4 * DIM], BF16, name="g_" + label, align_bytes=64)
+            codes = keep.tile([P, DIM], U32, name="c_" + label, align_bytes=64)
+            scales = keep.tile([P, DIM], U8, name="s_" + label, align_bytes=64)
+            g_words = grouped[:].bitcast(F32).rearrange("p (t u) -> p t u", u=2)
+            for half in range(2):
+                bank = transpose_half(src, half, stepped)
+                nc.scalar.copy(
+                    out=g_words[:, half * 256 : (half + 1) * 256, :],
+                    in_=bank[:].rearrange("p (u t) -> p t u", u=2),
+                )
+            nc.vector.quantize_mx(out=codes[:].bitcast(FP8X4), scales=scales[:], in_=grouped[:])
+            return codes, scales
+
+        h0g = {}
+        h0q = {}
+        h2g = {}
+        h2q = {}
+        y_t = {}
+
+        def valid(r):
+            return 0 <= r < ROUNDS
+
+        def x_half(r, half):
+            if half == 0:
+                h0g[r] = work.tile([P, 4 * ROUND], BF16, name="h0g", align_bytes=64)
+            bank = transpose_half(x_sb[r], half, False)
+            view = h0g[r][:].rearrange("p (t u e) -> p t u e", u=2, e=2)
+            nc.vector.tensor_tensor(
+                out=view[:, half * 256 : (half + 1) * 256, :, :],
+                in0=bank[:].bitcast(BF16).rearrange("p (u t e) -> p t u e", u=2, e=2),
+                in1=s0_t[:].unsqueeze(1).to_broadcast([P, 256, 2, 2]),
+                op=ALU.mult,
+            )
+
+        def quantise(grouped, label):
+            codes = work.tile([P, ROUND], U32, name="c_" + label, bufs=3, align_bytes=64)
+            scales = work.tile([P, ROUND], U8, name="s_" + label, bufs=3, align_bytes=64)
+            nc.vector.quantize_mx(out=codes[:].bitcast(FP8X4), scales=scales[:], in_=grouped[:])
+            return codes, scales
+
+        def first_matmul(r, i):
+            if i == 0:
+                h2g[r] = work.tile([P, 4 * ROUND], BF16, name="h2g", align_bytes=64)
+            codes, scales = h0q[r]
+            bank = new_bank()
+            for j in range(4):
+                nc.tensor.matmul_mx(
+                    out=bank[:, j * P : (j + 1) * P],
+                    lhsT=b_codes[:, j * P : (j + 1) * P].bitcast(FP8X4),
+                    lhsT_scale=b_scales[:, j * P : (j + 1) * P],
+                    rhs=codes[:, i * P : (i + 1) * P].bitcast(FP8X4),
+                    rhs_scale=scales[:, i * P : (i + 1) * P],
+                    start=True,
+                    stop=True,
+                )
+            view = h2g[r][:].rearrange("p (t j) -> p t j", j=4)
+            nc.vector.tensor_tensor(
+                out=view[:, i * P : (i + 1) * P, :],
+                in0=bank[:].rearrange("p (j t) -> p t j", j=4),
+                in1=s2_t[:].unsqueeze(1).to_broadcast([P, P, 4]),
+                op=ALU.mult,
+            )
+
+        def second_matmul(r, c):
+            if c == 0:
+                y_t[r] = work.tile([P, 4, ROUND], F32, name="y_t", bufs=3)
+            codes, scales = h2q[r]
+            bank = new_bank()
+            nc.tensor.matmul_mx(
+                out=bank[:],
+                lhsT=a_codes[:, c * P : (c + 1) * P].bitcast(FP8X4),
+                lhsT_scale=a_scales[:, c * P : (c + 1) * P],
+                rhs=codes[:].bitcast(FP8X4),
+                rhs_scale=scales[:],
+                start=True,
+                stop=True,
+            )
+            nc.scalar.activation(
+                out=y_t[r][:, c, :],
+                in_=bank[:],
+                func=ACT.Identity,
+                bias=bias_t[:, c : c + 1],
+                scale=s4_t[:, c : c + 1],
+            )
+
+        def finish(r):
+            o_sb = work.tile([P, 4, DIM], F32, name="o_sb", bufs=3)
+            for i in range(4):
+                bank = new_bank()
+                for c in range(4):
+                    nc.tensor.transpose(bank[:, c * P : (c + 1) * P], y_t[r][:, c, i * P : (i + 1) * P], ident[:])
+                nc.scalar.copy(out=o_sb[:, i, :], in_=bank[:])
+                if i % 2 == 1:
+                    nc.sync.dma_start(out=out_rounds[r][:, i - 1 : i + 1, :], in_=o_sb[:, i - 1 : i + 1, :])
+
+        b_codes, b_scales = prepare_weight(b_sb, False, "b")
+        a_codes, a_scales = None, None
+
+        for k in range(-2, ROUNDS + 2):
+            if valid(k + 2):
+                x_half(k + 2, 0)
+            if valid(k):
+                h2q[k] = quantise(h2g[k], "h2")
+            if valid(k + 2):
+                x_half(k + 2, 1)
+            if k == -1:
+                nc.vector.tensor_copy(out=s4_t[:], in_=s4_b[:])
+                nc.vector.tensor_copy(out=bias_t[:], in_=bias_b[:])
+                a_codes, a_scales = prepare_weight(a_sb, True, "a")
+            if valid(k - 2):
+                finish(k - 2)
+            for n in range(4):
+                if valid(k):
+                    second_matmul(k, n)
+                if valid(k + 1):
+                    first_matmul(k + 1, n)
+                if n == 0 and valid(k + 2):
+                    h0q[k + 2] = quantise(h0g[k + 2], "h0")

@@ -141,7 +141,7 @@ def tile_doublebinarylinear_t_kernel(tc, x, scaling0, B, scaling2, A, scaling4, 
 
         def second_matmul(r, c):
             if c == 0:
-                y_t[r] = work.tile([P, 4, ROUND], F32, name="y_t", bufs=3)
+                y_t[r] = work.tile([P, 4, ROUND], F32, name="y_t", bufs=4)
             codes, scales = h2q[r]
             bank = new_bank()
             nc.tensor.matmul_mx(
@@ -161,36 +161,35 @@ def tile_doublebinarylinear_t_kernel(tc, x, scaling0, B, scaling2, A, scaling4, 
                 scale=s4_t[:, c : c + 1],
             )
 
-        def finish(r):
-            o_sb = work.tile([P, 4, DIM], F32, name="o_sb", bufs=3)
-            for i in range(4):
+        def finish(r, half):
+            o_sb = work.tile([P, 2, DIM], F32, name="o_sb", bufs=6)
+            for il in range(2):
+                i = 2 * half + il
                 bank = new_bank()
                 for c in range(4):
                     nc.tensor.transpose(bank[:, c * P : (c + 1) * P], y_t[r][:, c, i * P : (i + 1) * P], ident[:])
-                nc.scalar.copy(out=o_sb[:, i, :], in_=bank[:])
-                if i % 2 == 1:
-                    nc.sync.dma_start(out=out_rounds[r][:, i - 1 : i + 1, :], in_=o_sb[:, i - 1 : i + 1, :])
+                nc.scalar.copy(out=o_sb[:, il, :], in_=bank[:])
+            nc.sync.dma_start(out=out_rounds[r][:, 2 * half : 2 * half + 2, :], in_=o_sb[:])
 
         b_codes, b_scales = prepare_weight(b_sb, False, "b")
         a_codes, a_scales = None, None
 
-        for k in range(-2, ROUNDS + 2):
-            if valid(k + 2):
-                x_half(k + 2, 0)
-            if valid(k):
-                h2q[k] = quantise(h2g[k], "h2")
-            if valid(k + 2):
-                x_half(k + 2, 1)
-            if k == -1:
-                nc.vector.tensor_copy(out=s4_t[:], in_=s4_b[:])
-                nc.vector.tensor_copy(out=bias_t[:], in_=bias_b[:])
-                a_codes, a_scales = prepare_weight(a_sb, True, "a")
-            if valid(k - 2):
-                finish(k - 2)
-            for n in range(4):
-                if valid(k):
-                    second_matmul(k, n)
-                if valid(k + 1):
-                    first_matmul(k + 1, n)
-                if n == 0 and valid(k + 2):
-                    h0q[k + 2] = quantise(h0g[k + 2], "h0")
+        for k in range(-2, ROUNDS + 3):
+            for half in range(2):
+                if valid(k + 2):
+                    x_half(k + 2, half)
+                if half == 0 and valid(k):
+                    h2q[k] = quantise(h2g[k], "h2")
+                if k == -1 and half == 0:
+                    nc.vector.tensor_copy(out=s4_t[:], in_=s4_b[:])
+                    nc.vector.tensor_copy(out=bias_t[:], in_=bias_b[:])
+                    a_codes, a_scales = prepare_weight(a_sb, True, "a")
+                if valid(k - 3):
+                    finish(k - 3, half)
+                for n in (2 * half, 2 * half + 1):
+                    if valid(k - 1):
+                        second_matmul(k - 1, n)
+                    if valid(k + 1):
+                        first_matmul(k + 1, n)
+                    if n == 2 and valid(k + 2):
+                        h0q[k + 2] = quantise(h0g[k + 2], "h0")

@@ -16,6 +16,9 @@ DIM = 512
 TOKENS = 4 * 2048
 ROUND = 512
 ROUNDS = TOKENS // ROUND
+UNITS = 2 * ROUNDS
+TAIL_EO = 3
+TAIL_E2 = 1
 FLOPS = 2 * 2 * TOKENS * DIM * DIM
 
 
@@ -95,39 +98,39 @@ def tile_doublebinarylinear_t_kernel(tc, x, scaling0, B, scaling2, A, scaling4, 
         h2q = {}
         y_t = {}
 
-        def valid(r):
-            return 0 <= r < ROUNDS
+        def unit_ok(u):
+            return 0 <= u < UNITS
 
-        def x_half(r, half):
-            if half == 0:
-                h0g[r] = work.tile([P, 4 * ROUND], BF16, name="h0g", align_bytes=64)
-            bank = transpose_half(x_sb[r], half, False)
-            view = h0g[r][:].rearrange("p (t u e) -> p t u e", u=2, e=2)
+        def x_unit(u):
+            h0g[u] = work.tile([P, 2 * ROUND], BF16, name="h0g", bufs=3, align_bytes=64)
+            bank = transpose_half(x_sb[u // 2], u % 2, False)
             nc.vector.tensor_tensor(
-                out=view[:, half * 256 : (half + 1) * 256, :, :],
+                out=h0g[u][:].rearrange("p (t u e) -> p t u e", u=2, e=2),
                 in0=bank[:].bitcast(BF16).rearrange("p (u t e) -> p t u e", u=2, e=2),
                 in1=s0_t[:].unsqueeze(1).to_broadcast([P, 256, 2, 2]),
                 op=ALU.mult,
             )
 
-        def quantise(grouped, label):
-            codes = work.tile([P, ROUND], U32, name="c_" + label, bufs=3, align_bytes=64)
-            scales = work.tile([P, ROUND], U8, name="s_" + label, bufs=3, align_bytes=64)
+        def quantise(grouped, width, label):
+            codes = work.tile([P, width], U32, name="c_" + label, bufs=4, align_bytes=64)
+            scales = work.tile([P, width], U8, name="s_" + label, bufs=4, align_bytes=64)
             nc.vector.quantize_mx(out=codes[:].bitcast(FP8X4), scales=scales[:], in_=grouped[:])
             return codes, scales
 
-        def first_matmul(r, i):
+        def first_matmul(u, il):
+            r = u // 2
+            i = 2 * (u % 2) + il
             if i == 0:
-                h2g[r] = work.tile([P, 4 * ROUND], BF16, name="h2g", align_bytes=64)
-            codes, scales = h0q[r]
+                h2g[r] = work.tile([P, 4 * ROUND], BF16, name="h2g", bufs=3, align_bytes=64)
+            codes, scales = h0q[u]
             bank = new_bank()
             for j in range(4):
                 nc.tensor.matmul_mx(
                     out=bank[:, j * P : (j + 1) * P],
                     lhsT=b_codes[:, j * P : (j + 1) * P].bitcast(FP8X4),
                     lhsT_scale=b_scales[:, j * P : (j + 1) * P],
-                    rhs=codes[:, i * P : (i + 1) * P].bitcast(FP8X4),
-                    rhs_scale=scales[:, i * P : (i + 1) * P],
+                    rhs=codes[:, il * P : (il + 1) * P].bitcast(FP8X4),
+                    rhs_scale=scales[:, il * P : (il + 1) * P],
                     start=True,
                     stop=True,
                 )
@@ -153,43 +156,57 @@ def tile_doublebinarylinear_t_kernel(tc, x, scaling0, B, scaling2, A, scaling4, 
                 start=True,
                 stop=True,
             )
-            nc.scalar.activation(
-                out=y_t[r][:, c, :],
-                in_=bank[:],
-                func=ACT.Identity,
-                bias=bias_t[:, c : c + 1],
-                scale=s4_t[:, c : c + 1],
-            )
+            if r >= ROUNDS - TAIL_E2 and c % 2 == 1:
+                nc.vector.tensor_scalar(
+                    out=y_t[r][:, c, :],
+                    in0=bank[:],
+                    scalar1=s4_t[:, c : c + 1],
+                    scalar2=bias_t[:, c : c + 1],
+                    op0=ALU.mult,
+                    op1=ALU.add,
+                )
+            else:
+                nc.scalar.activation(
+                    out=y_t[r][:, c, :],
+                    in_=bank[:],
+                    func=ACT.Identity,
+                    bias=bias_t[:, c : c + 1],
+                    scale=s4_t[:, c : c + 1],
+                )
 
-        def finish(r, half):
+        def finish(u):
+            r = u // 2
+            half = u % 2
             o_sb = work.tile([P, 2, DIM], F32, name="o_sb", bufs=6)
             for il in range(2):
                 i = 2 * half + il
                 bank = new_bank()
                 for c in range(4):
                     nc.tensor.transpose(bank[:, c * P : (c + 1) * P], y_t[r][:, c, i * P : (i + 1) * P], ident[:])
-                nc.scalar.copy(out=o_sb[:, il, :], in_=bank[:])
+                if r >= ROUNDS - TAIL_EO and il == 1:
+                    nc.vector.tensor_copy(out=o_sb[:, il, :], in_=bank[:])
+                else:
+                    nc.scalar.copy(out=o_sb[:, il, :], in_=bank[:])
             nc.sync.dma_start(out=out_rounds[r][:, 2 * half : 2 * half + 2, :], in_=o_sb[:])
 
         b_codes, b_scales = prepare_weight(b_sb, False, "b")
         a_codes, a_scales = None, None
 
-        for k in range(-2, ROUNDS + 3):
-            for half in range(2):
-                if valid(k + 2):
-                    x_half(k + 2, half)
-                if half == 0 and valid(k):
-                    h2q[k] = quantise(h2g[k], "h2")
-                if k == -1 and half == 0:
-                    nc.vector.tensor_copy(out=s4_t[:], in_=s4_b[:])
-                    nc.vector.tensor_copy(out=bias_t[:], in_=bias_b[:])
-                    a_codes, a_scales = prepare_weight(a_sb, True, "a")
-                if valid(k - 3):
-                    finish(k - 3, half)
-                for n in (2 * half, 2 * half + 1):
-                    if valid(k - 1):
-                        second_matmul(k - 1, n)
-                    if valid(k + 1):
-                        first_matmul(k + 1, n)
-                    if n == 2 and valid(k + 2):
-                        h0q[k + 2] = quantise(h0g[k + 2], "h0")
+        for s in range(-3, UNITS + 5):
+            if unit_ok(s + 3):
+                x_unit(s + 3)
+            if unit_ok(s + 2):
+                h0q[s + 2] = quantise(h0g[s + 2], ROUND // 2, "h0")
+            if s % 2 == 1 and unit_ok(s - 1):
+                h2q[(s - 1) // 2] = quantise(h2g[(s - 1) // 2], ROUND, "h2")
+            if s == 0:
+                nc.scalar.copy(out=s4_t[:], in_=s4_b[:])
+                nc.scalar.copy(out=bias_t[:], in_=bias_b[:])
+                a_codes, a_scales = prepare_weight(a_sb, True, "a")
+            if unit_ok(s - 5):
+                finish(s - 5)
+            for n in range(2):
+                if unit_ok(s - 2):
+                    second_matmul((s - 2) // 2, 2 * ((s - 2) % 2) + n)
+                if unit_ok(s + 1):
+                    first_matmul(s + 1, n)

@@ -39,19 +39,26 @@ def tile_doublebinarylinear_t_kernel(tc, x, scaling0, B, scaling2, A, scaling4, 
         bias_b = keep.tile([P, 4], BF16, name="bias_b")
         nc.scalar.dma_start(out=s0_t[:], in_=scaling0.rearrange("(u p e) -> p u e", u=2, e=2))
         nc.scalar.dma_start(out=s2_t[:], in_=scaling2.rearrange("(q j) -> q j", j=4))
-        with nc.allow_non_contiguous_dma(reason="two vectors of 512 values, one value a partition and chunk"):
-            nc.scalar.dma_start(out=s4_b[:], in_=scaling4.rearrange("(c r) -> r c", c=4))
-            nc.scalar.dma_start(out=bias_b[:], in_=bias.rearrange("(c r) -> r c", c=4))
 
         b_sb = keep.tile([P, 4, DIM], BF16, name="b_sb")
         a_sb = keep.tile([P, 4, DIM], BF16, name="a_sb")
-        x_sb = [keep.tile([P, 4, DIM], BF16, name="x_sb%d" % r) for r in range(ROUNDS)]
+        x_first = [keep.tile([P, 2, DIM], BF16, name="x_first%d" % u) for u in range(2)]
+        x_sb = [keep.tile([P, 4, DIM], BF16, name="x_sb%d" % r) for r in range(1, ROUNDS)]
+        nc.sync.dma_start(out=x_first[0][:], in_=x_rounds[0][:, 0:2, :])
         nc.sync.dma_start(out=b_sb[:], in_=B.rearrange("(q j) k -> q j k", j=4))
-        nc.sync.dma_start(out=x_sb[0][:], in_=x_rounds[0])
-        nc.sync.dma_start(out=x_sb[1][:], in_=x_rounds[1])
+        nc.sync.dma_start(out=x_first[1][:], in_=x_rounds[0][:, 2:4, :])
+        nc.sync.dma_start(out=x_sb[0][:], in_=x_rounds[1])
         nc.sync.dma_start(out=a_sb[:], in_=A.rearrange("(c r) m -> r c m", c=4))
+        with nc.allow_non_contiguous_dma(reason="two vectors of 512 values, one value a partition and chunk"):
+            nc.sync.dma_start(out=s4_b[:], in_=scaling4.rearrange("(c r) -> r c", c=4))
+            nc.sync.dma_start(out=bias_b[:], in_=bias.rearrange("(c r) -> r c", c=4))
         for r in range(2, ROUNDS):
-            nc.sync.dma_start(out=x_sb[r][:], in_=x_rounds[r])
+            nc.sync.dma_start(out=x_sb[r - 1][:], in_=x_rounds[r])
+
+        warm_in = keep.tile([P, 1], F32, name="warm_in")
+        warm_out = keep.tile([P, 1], F32, name="warm_out")
+        nc.vector.memset(warm_in[:], 0.0)
+        nc.scalar.copy(out=warm_out[:], in_=warm_in[:])
 
         ident = keep.tile([P, P], F32, name="ident")
         make_identity(nc, ident[:])
@@ -78,17 +85,23 @@ def tile_doublebinarylinear_t_kernel(tc, x, scaling0, B, scaling2, A, scaling4, 
                     nc.tensor.transpose(bank[:, col : col + P], block, ident[:])
             return bank
 
-        def prepare_weight(src, stepped, label):
+        def prepare_weight(src, stepped, share, label):
             grouped = keep.tile([P, 4 * DIM], BF16, name="g_" + label, align_bytes=64)
             codes = keep.tile([P, DIM], U32, name="c_" + label, align_bytes=64)
             scales = keep.tile([P, DIM], U8, name="s_" + label, align_bytes=64)
             g_words = grouped[:].bitcast(F32).rearrange("p (t u) -> p t u", u=2)
             for half in range(2):
                 bank = transpose_half(src, half, stepped)
-                nc.scalar.copy(
-                    out=g_words[:, half * 256 : (half + 1) * 256, :],
-                    in_=bank[:].rearrange("p (u t) -> p t u", u=2),
-                )
+                if half == 0 and share:
+                    nc.vector.tensor_copy(
+                        out=g_words[:, half * 256 : (half + 1) * 256, :],
+                        in_=bank[:].rearrange("p (u t) -> p t u", u=2),
+                    )
+                else:
+                    nc.scalar.copy(
+                        out=g_words[:, half * 256 : (half + 1) * 256, :],
+                        in_=bank[:].rearrange("p (u t) -> p t u", u=2),
+                    )
             nc.vector.quantize_mx(out=codes[:].bitcast(FP8X4), scales=scales[:], in_=grouped[:])
             return codes, scales
 
@@ -103,7 +116,10 @@ def tile_doublebinarylinear_t_kernel(tc, x, scaling0, B, scaling2, A, scaling4, 
 
         def x_unit(u):
             h0g[u] = work.tile([P, 2 * ROUND], BF16, name="h0g", bufs=3, align_bytes=64)
-            bank = transpose_half(x_sb[u // 2], u % 2, False)
+            if u < 2:
+                bank = transpose_half(x_first[u], 0, False)
+            else:
+                bank = transpose_half(x_sb[u // 2 - 1], u % 2, False)
             nc.vector.tensor_tensor(
                 out=h0g[u][:].rearrange("p (t u e) -> p t u e", u=2, e=2),
                 in0=bank[:].bitcast(BF16).rearrange("p (u t e) -> p t u e", u=2, e=2),
@@ -187,14 +203,19 @@ def tile_doublebinarylinear_t_kernel(tc, x, scaling0, B, scaling2, A, scaling4, 
                     nc.vector.tensor_copy(out=o_sb[:, il, :], in_=bank[:])
                 else:
                     nc.scalar.copy(out=o_sb[:, il, :], in_=bank[:])
-            nc.sync.dma_start(out=out_rounds[r][:, 2 * half : 2 * half + 2, :], in_=o_sb[:])
+                if u == UNITS - 1:
+                    nc.sync.dma_start(out=out_rounds[r][:, i : i + 1, :], in_=o_sb[:, il : il + 1, :])
+            if u < UNITS - 1:
+                nc.sync.dma_start(out=out_rounds[r][:, 2 * half : 2 * half + 2, :], in_=o_sb[:])
 
-        b_codes, b_scales = prepare_weight(b_sb, False, "b")
+        b_codes, b_scales = None, None
         a_codes, a_scales = None, None
 
         for s in range(-3, UNITS + 5):
             if unit_ok(s + 3):
                 x_unit(s + 3)
+            if s == -3:
+                b_codes, b_scales = prepare_weight(b_sb, False, True, "b")
             if unit_ok(s + 2):
                 h0q[s + 2] = quantise(h0g[s + 2], ROUND // 2, "h0")
             if s % 2 == 1 and unit_ok(s - 1):
@@ -202,7 +223,7 @@ def tile_doublebinarylinear_t_kernel(tc, x, scaling0, B, scaling2, A, scaling4, 
             if s == 0:
                 nc.scalar.copy(out=s4_t[:], in_=s4_b[:])
                 nc.scalar.copy(out=bias_t[:], in_=bias_b[:])
-                a_codes, a_scales = prepare_weight(a_sb, True, "a")
+                a_codes, a_scales = prepare_weight(a_sb, True, False, "a")
             if unit_ok(s - 5):
                 finish(s - 5)
             for n in range(2):

@@ -17,7 +17,18 @@ TOKENS = 4 * 2048
 ROUND = 512
 ROUNDS = TOKENS // ROUND
 UNITS = 2 * ROUNDS
-TAIL_EO = 3
+UNIT = ROUND // 2
+FIN = 3
+DQ = 0
+M2 = 1
+AW = 0
+ROWS = 2
+QP = 4
+QR = 3
+Q0 = 6
+Q1 = 30
+GL = 2
+TAIL_EO = 4
 TAIL_E2 = 1
 FLOPS = 2 * 2 * TOKENS * DIM * DIM
 
@@ -65,6 +76,11 @@ def tile_doublebinarylinear_t_kernel(tc, x, scaling0, B, scaling2, A, scaling4, 
         s4_t = keep.tile([P, 4], F32, name="s4_t")
         bias_t = keep.tile([P, 4], F32, name="bias_t")
 
+        ident_b = keep.tile([P, P], BF16, name="ident_b")
+        nc.scalar.copy(out=ident_b[:], in_=ident[:])
+        s4_row = keep.tile([P, DIM], F32, name="s4_row")
+        bias_row = keep.tile([P, DIM], F32, name="bias_row")
+
         banks_made = []
 
         def new_bank():
@@ -84,6 +100,18 @@ def tile_doublebinarylinear_t_kernel(tc, x, scaling0, B, scaling2, A, scaling4, 
                     col = (2 * u + il) * P
                     nc.tensor.transpose(bank[:, col : col + P], block, ident[:])
             return bank
+
+        def spread_row(row, column):
+            bank = new_bank()
+            for c in range(4):
+                nc.tensor.matmul(
+                    bank[:, c * P : (c + 1) * P],
+                    lhsT=column[:, c : c + 1].to_broadcast([P, P]),
+                    rhs=ident_b[:],
+                    start=True,
+                    stop=True,
+                )
+            nc.scalar.copy(out=row[:], in_=bank[:])
 
         def prepare_weight(src, stepped, share, label):
             grouped = keep.tile([P, 4 * DIM], BF16, name="g_" + label, align_bytes=64)
@@ -134,10 +162,8 @@ def tile_doublebinarylinear_t_kernel(tc, x, scaling0, B, scaling2, A, scaling4, 
             return codes, scales
 
         def first_matmul(u, il):
-            r = u // 2
-            i = 2 * (u % 2) + il
-            if i == 0:
-                h2g[r] = work.tile([P, 4 * ROUND], BF16, name="h2g", bufs=3, align_bytes=64)
+            if il == 0:
+                h2g[u] = work.tile([P, 4 * UNIT], BF16, name="h2g", bufs=4, align_bytes=64)
             codes, scales = h0q[u]
             bank = new_bank()
             for j in range(4):
@@ -150,32 +176,19 @@ def tile_doublebinarylinear_t_kernel(tc, x, scaling0, B, scaling2, A, scaling4, 
                     start=True,
                     stop=True,
                 )
-            view = h2g[r][:].rearrange("p (t j) -> p t j", j=4)
+            view = h2g[u][:].rearrange("p (t j) -> p t j", j=4)
             nc.vector.tensor_tensor(
-                out=view[:, i * P : (i + 1) * P, :],
+                out=view[:, il * P : (il + 1) * P, :],
                 in0=bank[:].rearrange("p (j t) -> p t j", j=4),
                 in1=s2_t[:].unsqueeze(1).to_broadcast([P, P, 4]),
                 op=ALU.mult,
             )
 
-        def second_matmul(r, c):
-            if c == 0:
-                y_t[r] = work.tile([P, 4, ROUND], F32, name="y_t", bufs=4)
-            codes, scales = h2q[r]
-            bank = new_bank()
-            nc.tensor.matmul_mx(
-                out=bank[:],
-                lhsT=a_codes[:, c * P : (c + 1) * P].bitcast(FP8X4),
-                lhsT_scale=a_scales[:, c * P : (c + 1) * P],
-                rhs=codes[:].bitcast(FP8X4),
-                rhs_scale=scales[:],
-                start=True,
-                stop=True,
-            )
-            if r >= ROUNDS - TAIL_E2 and c % 2 == 1:
+        def scale_and_bias(eng, u, c, src):
+            if eng == "v":
                 nc.vector.tensor_scalar(
-                    out=y_t[r][:, c, :],
-                    in0=bank[:],
+                    out=y_t[u][:, c, :],
+                    in0=src,
                     scalar1=s4_t[:, c : c + 1],
                     scalar2=bias_t[:, c : c + 1],
                     op0=ALU.mult,
@@ -183,12 +196,62 @@ def tile_doublebinarylinear_t_kernel(tc, x, scaling0, B, scaling2, A, scaling4, 
                 )
             else:
                 nc.scalar.activation(
-                    out=y_t[r][:, c, :],
-                    in_=bank[:],
+                    out=y_t[u][:, c, :],
+                    in_=src,
                     func=ACT.Identity,
                     bias=bias_t[:, c : c + 1],
                     scale=s4_t[:, c : c + 1],
                 )
+
+        def second_matmul(u, pair):
+            if pair == 0:
+                y_t[u] = work.tile([P, 4, UNIT], F32, name="y_t", bufs=4)
+            codes, scales = h2q[u]
+            bank = new_bank()
+            for k in range(2):
+                c = 2 * pair + k
+                nc.tensor.matmul_mx(
+                    out=bank[:, k * UNIT : (k + 1) * UNIT],
+                    lhsT=a_codes[:, c * P : (c + 1) * P].bitcast(FP8X4),
+                    lhsT_scale=a_scales[:, c * P : (c + 1) * P],
+                    rhs=codes[:].bitcast(FP8X4),
+                    rhs_scale=scales[:],
+                    start=True,
+                    stop=True,
+                )
+            for k in range(2):
+                scale_and_bias("v" if u >= UNITS - TAIL_E2 and pair == 1 else "s", u, 2 * pair + k, bank[:, k * UNIT : (k + 1) * UNIT])
+
+        def flat(u):
+            return Q0 <= u < Q1 and u % QP == QR
+
+        raw = {}
+        scaled = {}
+
+        def token_matmul(u, il):
+            codes, scales = h2q[u]
+            bank = new_bank()
+            nc.tensor.matmul_mx(
+                out=bank[:],
+                lhsT=codes[:, il * P : (il + 1) * P].bitcast(FP8X4),
+                lhsT_scale=scales[:, il * P : (il + 1) * P],
+                rhs=a_codes[:].bitcast(FP8X4),
+                rhs_scale=a_scales[:],
+                start=True,
+                stop=True,
+            )
+            raw[u, il] = work.tile([P, DIM], F32, name="raw", bufs=4)
+            nc.scalar.copy(out=raw[u, il][:], in_=bank[:])
+
+        def flat_step(u, k):
+            il = k // 2
+            if k % 2 == 0:
+                scaled[u, il] = work.tile([P, DIM], F32, name="scaled", bufs=3)
+                nc.gpsimd.tensor_tensor(out=scaled[u, il][:], in0=raw[u, il][:], in1=s4_row[:], op=ALU.mult)
+            else:
+                o_g = work.tile([P, DIM], F32, name="o_g", bufs=4)
+                nc.gpsimd.tensor_tensor(out=o_g[:], in0=scaled[u, il][:], in1=bias_row[:], op=ALU.add)
+                nc.sync.dma_start(out=out_rounds[u // 2][:, 2 * (u % 2) + il, :], in_=o_g[:])
 
         def finish(u):
             r = u // 2
@@ -198,8 +261,8 @@ def tile_doublebinarylinear_t_kernel(tc, x, scaling0, B, scaling2, A, scaling4, 
                 i = 2 * half + il
                 bank = new_bank()
                 for c in range(4):
-                    nc.tensor.transpose(bank[:, c * P : (c + 1) * P], y_t[r][:, c, i * P : (i + 1) * P], ident[:])
-                if r >= ROUNDS - TAIL_EO and il == 1:
+                    nc.tensor.transpose(bank[:, c * P : (c + 1) * P], y_t[u][:, c, il * P : (il + 1) * P], ident[:])
+                if u >= UNITS - TAIL_EO and il == 1:
                     nc.vector.tensor_copy(out=o_sb[:, il, :], in_=bank[:])
                 else:
                     nc.scalar.copy(out=o_sb[:, il, :], in_=bank[:])
@@ -211,23 +274,32 @@ def tile_doublebinarylinear_t_kernel(tc, x, scaling0, B, scaling2, A, scaling4, 
         b_codes, b_scales = None, None
         a_codes, a_scales = None, None
 
-        for s in range(-3, UNITS + 5):
+        for s in range(-3, UNITS + 8):
             if unit_ok(s + 3):
                 x_unit(s + 3)
             if s == -3:
                 b_codes, b_scales = prepare_weight(b_sb, False, True, "b")
             if unit_ok(s + 2):
-                h0q[s + 2] = quantise(h0g[s + 2], ROUND // 2, "h0")
-            if s % 2 == 1 and unit_ok(s - 1):
-                h2q[(s - 1) // 2] = quantise(h2g[(s - 1) // 2], ROUND, "h2")
-            if s == 0:
+                h0q[s + 2] = quantise(h0g[s + 2], UNIT, "h0")
+            if unit_ok(s - DQ):
+                h2q[s - DQ] = quantise(h2g[s - DQ], UNIT, "h2")
+            if s == AW:
                 nc.scalar.copy(out=s4_t[:], in_=s4_b[:])
                 nc.scalar.copy(out=bias_t[:], in_=bias_b[:])
                 a_codes, a_scales = prepare_weight(a_sb, True, False, "a")
-            if unit_ok(s - 5):
-                finish(s - 5)
+            if unit_ok(s - FIN) and not flat(s - FIN):
+                finish(s - FIN)
+            for k in range(4):
+                if unit_ok(s - GL - k) and flat(s - GL - k):
+                    flat_step(s - GL - k, k)
+            if s == ROWS:
+                spread_row(s4_row, s4_b)
+                spread_row(bias_row, bias_b)
             for n in range(2):
-                if unit_ok(s - 2):
-                    second_matmul((s - 2) // 2, 2 * ((s - 2) % 2) + n)
+                if unit_ok(s - M2):
+                    if flat(s - M2):
+                        token_matmul(s - M2, n)
+                    else:
+                        second_matmul(s - M2, n)
                 if unit_ok(s + 1):
                     first_matmul(s + 1, n)

@@ -23,11 +23,12 @@ DQ = 0
 M2 = 1
 AW = 0
 ROWS = 2
+MIDS = 6
 QP = 4
 QR = 3
 Q0 = 6
 Q1 = 30
-GL = 2
+GL = 3
 TAIL_EO = 4
 TAIL_E2 = 1
 FLOPS = 2 * 2 * TOKENS * DIM * DIM
@@ -163,7 +164,7 @@ def tile_doublebinarylinear_t_kernel(tc, x, scaling0, B, scaling2, A, scaling4, 
 
         def first_matmul(u, il):
             if il == 0:
-                h2g[u] = work.tile([P, 4 * UNIT], BF16, name="h2g", bufs=4, align_bytes=64)
+                h2g[u] = work.tile([P, 4 * UNIT], BF16, name="h2g", tag="mid%d" % (u % MIDS), bufs=1, align_bytes=64)
             codes, scales = h0q[u]
             bank = new_bank()
             for j in range(4):
@@ -243,13 +244,13 @@ def tile_doublebinarylinear_t_kernel(tc, x, scaling0, B, scaling2, A, scaling4, 
             raw[u, il] = work.tile([P, DIM], F32, name="raw", bufs=4)
             nc.scalar.copy(out=raw[u, il][:], in_=bank[:])
 
-        def flat_step(u, k):
+        def flat_step(u, k, s):
             il = k // 2
             if k % 2 == 0:
-                scaled[u, il] = work.tile([P, DIM], F32, name="scaled", bufs=3)
+                scaled[u, il] = work.tile([P, DIM], F32, name="scaled", tag="mid%d" % (s % MIDS), bufs=1, align_bytes=64)
                 nc.gpsimd.tensor_tensor(out=scaled[u, il][:], in0=raw[u, il][:], in1=s4_row[:], op=ALU.mult)
             else:
-                o_g = work.tile([P, DIM], F32, name="o_g", bufs=4)
+                o_g = work.tile([P, DIM], F32, name="o_g", tag="mid%d" % (s % MIDS), bufs=1, align_bytes=64)
                 nc.gpsimd.tensor_tensor(out=o_g[:], in0=scaled[u, il][:], in1=bias_row[:], op=ALU.add)
                 nc.sync.dma_start(out=out_rounds[u // 2][:, 2 * (u % 2) + il, :], in_=o_g[:])
 
@@ -291,7 +292,7 @@ def tile_doublebinarylinear_t_kernel(tc, x, scaling0, B, scaling2, A, scaling4, 
                 finish(s - FIN)
             for k in range(4):
                 if unit_ok(s - GL - k) and flat(s - GL - k):
-                    flat_step(s - GL - k, k)
+                    flat_step(s - GL - k, k, s)
             if s == ROWS:
                 spread_row(s4_row, s4_b)
                 spread_row(bias_row, bias_b)

@@ -22,13 +22,6 @@ FIN = 3
 DQ = 0
 M2 = 1
 AW = 0
-ROWS = 2
-MIDS = 6
-QP = 4
-QR = 3
-Q0 = 6
-Q1 = 30
-GL = 3
 TAIL_EO = 4
 TAIL_E2 = 1
 FLOPS = 2 * 2 * TOKENS * DIM * DIM
@@ -77,11 +70,6 @@ def tile_doublebinarylinear_t_kernel(tc, x, scaling0, B, scaling2, A, scaling4, 
         s4_t = keep.tile([P, 4], F32, name="s4_t")
         bias_t = keep.tile([P, 4], F32, name="bias_t")
 
-        ident_b = keep.tile([P, P], BF16, name="ident_b")
-        nc.scalar.copy(out=ident_b[:], in_=ident[:])
-        s4_row = keep.tile([P, DIM], F32, name="s4_row")
-        bias_row = keep.tile([P, DIM], F32, name="bias_row")
-
         banks_made = []
 
         def new_bank():
@@ -101,18 +89,6 @@ def tile_doublebinarylinear_t_kernel(tc, x, scaling0, B, scaling2, A, scaling4, 
                     col = (2 * u + il) * P
                     nc.tensor.transpose(bank[:, col : col + P], block, ident[:])
             return bank
-
-        def spread_row(row, column):
-            bank = new_bank()
-            for c in range(4):
-                nc.tensor.matmul(
-                    bank[:, c * P : (c + 1) * P],
-                    lhsT=column[:, c : c + 1].to_broadcast([P, P]),
-                    rhs=ident_b[:],
-                    start=True,
-                    stop=True,
-                )
-            nc.scalar.copy(out=row[:], in_=bank[:])
 
         def prepare_weight(src, stepped, share, label):
             grouped = keep.tile([P, 4 * DIM], BF16, name="g_" + label, align_bytes=64)
@@ -164,7 +140,7 @@ def tile_doublebinarylinear_t_kernel(tc, x, scaling0, B, scaling2, A, scaling4, 
 
         def first_matmul(u, il):
             if il == 0:
-                h2g[u] = work.tile([P, 4 * UNIT], BF16, name="h2g", tag="mid%d" % (u % MIDS), bufs=1, align_bytes=64)
+                h2g[u] = work.tile([P, 4 * UNIT], BF16, name="h2g", bufs=4, align_bytes=64)
             codes, scales = h0q[u]
             bank = new_bank()
             for j in range(4):
@@ -223,37 +199,6 @@ def tile_doublebinarylinear_t_kernel(tc, x, scaling0, B, scaling2, A, scaling4, 
             for k in range(2):
                 scale_and_bias("v" if u >= UNITS - TAIL_E2 and pair == 1 else "s", u, 2 * pair + k, bank[:, k * UNIT : (k + 1) * UNIT])
 
-        def flat(u):
-            return Q0 <= u < Q1 and u % QP == QR
-
-        raw = {}
-        scaled = {}
-
-        def token_matmul(u, il):
-            codes, scales = h2q[u]
-            bank = new_bank()
-            nc.tensor.matmul_mx(
-                out=bank[:],
-                lhsT=codes[:, il * P : (il + 1) * P].bitcast(FP8X4),
-                lhsT_scale=scales[:, il * P : (il + 1) * P],
-                rhs=a_codes[:].bitcast(FP8X4),
-                rhs_scale=a_scales[:],
-                start=True,
-                stop=True,
-            )
-            raw[u, il] = work.tile([P, DIM], F32, name="raw", bufs=4)
-            nc.scalar.copy(out=raw[u, il][:], in_=bank[:])
-
-        def flat_step(u, k, s):
-            il = k // 2
-            if k % 2 == 0:
-                scaled[u, il] = work.tile([P, DIM], F32, name="scaled", tag="mid%d" % (s % MIDS), bufs=1, align_bytes=64)
-                nc.gpsimd.tensor_tensor(out=scaled[u, il][:], in0=raw[u, il][:], in1=s4_row[:], op=ALU.mult)
-            else:
-                o_g = work.tile([P, DIM], F32, name="o_g", tag="mid%d" % (s % MIDS), bufs=1, align_bytes=64)
-                nc.gpsimd.tensor_tensor(out=o_g[:], in0=scaled[u, il][:], in1=bias_row[:], op=ALU.add)
-                nc.sync.dma_start(out=out_rounds[u // 2][:, 2 * (u % 2) + il, :], in_=o_g[:])
-
         def finish(u):
             r = u // 2
             half = u % 2
@@ -275,7 +220,7 @@ def tile_doublebinarylinear_t_kernel(tc, x, scaling0, B, scaling2, A, scaling4, 
         b_codes, b_scales = None, None
         a_codes, a_scales = None, None
 
-        for s in range(-3, UNITS + 8):
+        for s in range(-3, UNITS + FIN):
             if unit_ok(s + 3):
                 x_unit(s + 3)
             if s == -3:
@@ -288,19 +233,10 @@ def tile_doublebinarylinear_t_kernel(tc, x, scaling0, B, scaling2, A, scaling4, 
                 nc.scalar.copy(out=s4_t[:], in_=s4_b[:])
                 nc.scalar.copy(out=bias_t[:], in_=bias_b[:])
                 a_codes, a_scales = prepare_weight(a_sb, True, False, "a")
-            if unit_ok(s - FIN) and not flat(s - FIN):
+            if unit_ok(s - FIN):
                 finish(s - FIN)
-            for k in range(4):
-                if unit_ok(s - GL - k) and flat(s - GL - k):
-                    flat_step(s - GL - k, k, s)
-            if s == ROWS:
-                spread_row(s4_row, s4_b)
-                spread_row(bias_row, bias_b)
             for n in range(2):
                 if unit_ok(s - M2):
-                    if flat(s - M2):
-                        token_matmul(s - M2, n)
-                    else:
-                        second_matmul(s - M2, n)
+                    second_matmul(s - M2, n)
                 if unit_ok(s + 1):
                     first_matmul(s + 1, n)

@@ -14,16 +14,12 @@ ALU = mybir.AluOpType
 P = 128
 DIM = 512
 TOKENS = 4 * 2048
-ROUND = 512
-ROUNDS = TOKENS // ROUND
+UNIT = 256
+ROUNDS = TOKENS // (2 * UNIT)
 UNITS = 2 * ROUNDS
-UNIT = ROUND // 2
-FIN = 3
-DQ = 0
-M2 = 1
-AW = 0
-TAIL_EO = 4
-TAIL_E2 = 1
+TAIL_EO = 5
+TAIL_E2 = 2
+FINE = 2
 FLOPS = 2 * 2 * TOKENS * DIM * DIM
 
 
@@ -39,18 +35,20 @@ def tile_doublebinarylinear_t_kernel(tc, x, scaling0, B, scaling2, A, scaling4, 
         psum = ctx.enter_context(tc.psum_pool(name="psum", bufs=1))
 
         s0_t = keep.tile([P, 2, 2], BF16, name="s0_t")
-        s2_t = keep.tile([P, 4], BF16, name="s2_t")
+        s2_t = keep.tile([P, 2, 2], BF16, name="s2_t")
         s4_b = keep.tile([P, 4], BF16, name="s4_b")
         bias_b = keep.tile([P, 4], BF16, name="bias_b")
         nc.scalar.dma_start(out=s0_t[:], in_=scaling0.rearrange("(u p e) -> p u e", u=2, e=2))
-        nc.scalar.dma_start(out=s2_t[:], in_=scaling2.rearrange("(q j) -> q j", j=4))
+        nc.scalar.dma_start(out=s2_t[:], in_=scaling2.rearrange("(u q e) -> q u e", u=2, e=2))
 
         b_sb = keep.tile([P, 4, DIM], BF16, name="b_sb")
         a_sb = keep.tile([P, 4, DIM], BF16, name="a_sb")
         x_first = [keep.tile([P, 2, DIM], BF16, name="x_first%d" % u) for u in range(2)]
         x_sb = [keep.tile([P, 4, DIM], BF16, name="x_sb%d" % r) for r in range(1, ROUNDS)]
+        b_view = B.rearrange("(u q e) k -> q u e k", u=2, e=2)
         nc.sync.dma_start(out=x_first[0][:], in_=x_rounds[0][:, 0:2, :])
-        nc.sync.dma_start(out=b_sb[:], in_=B.rearrange("(q j) k -> q j k", j=4))
+        for u in range(2):
+            nc.sync.dma_start(out=b_sb[:, 2 * u : 2 * u + 2, :], in_=b_view[:, u, :, :])
         nc.sync.dma_start(out=x_first[1][:], in_=x_rounds[0][:, 2:4, :])
         nc.sync.dma_start(out=x_sb[0][:], in_=x_rounds[1])
         nc.sync.dma_start(out=a_sb[:], in_=A.rearrange("(c r) m -> r c m", c=4))
@@ -77,36 +75,27 @@ def tile_doublebinarylinear_t_kernel(tc, x, scaling0, B, scaling2, A, scaling4, 
             banks_made.append(n)
             return psum.tile([P, 512], F32, name="bank%d" % n, tag="bank%d" % n)
 
-        def transpose_half(src, half, stepped):
+        def transpose_half(src, half):
             bank = new_bank()
             for u in range(2):
                 for il in range(2):
                     words = src[:, 2 * half + il, :].bitcast(F32)
-                    if stepped:
-                        block = words.rearrange("p (q u) -> p u q", u=2)[:, u, :]
-                    else:
-                        block = words[:, u * P : (u + 1) * P]
                     col = (2 * u + il) * P
-                    nc.tensor.transpose(bank[:, col : col + P], block, ident[:])
+                    nc.tensor.transpose(bank[:, col : col + P], words[:, u * P : (u + 1) * P], ident[:])
             return bank
 
-        def prepare_weight(src, stepped, share, label):
+        def prepare_weight(src, share, label):
             grouped = keep.tile([P, 4 * DIM], BF16, name="g_" + label, align_bytes=64)
             codes = keep.tile([P, DIM], U32, name="c_" + label, align_bytes=64)
             scales = keep.tile([P, DIM], U8, name="s_" + label, align_bytes=64)
             g_words = grouped[:].bitcast(F32).rearrange("p (t u) -> p t u", u=2)
             for half in range(2):
-                bank = transpose_half(src, half, stepped)
+                bank = transpose_half(src, half)
+                words = bank[:].rearrange("p (u t) -> p t u", u=2)
                 if half == 0 and share:
-                    nc.vector.tensor_copy(
-                        out=g_words[:, half * 256 : (half + 1) * 256, :],
-                        in_=bank[:].rearrange("p (u t) -> p t u", u=2),
-                    )
+                    nc.vector.tensor_copy(out=g_words[:, half * 256 : (half + 1) * 256, :], in_=words)
                 else:
-                    nc.scalar.copy(
-                        out=g_words[:, half * 256 : (half + 1) * 256, :],
-                        in_=bank[:].rearrange("p (u t) -> p t u", u=2),
-                    )
+                    nc.scalar.copy(out=g_words[:, half * 256 : (half + 1) * 256, :], in_=words)
             nc.vector.quantize_mx(out=codes[:].bitcast(FP8X4), scales=scales[:], in_=grouped[:])
             return codes, scales
 
@@ -120,21 +109,18 @@ def tile_doublebinarylinear_t_kernel(tc, x, scaling0, B, scaling2, A, scaling4, 
             return 0 <= u < UNITS
 
         def x_unit(u):
-            h0g[u] = work.tile([P, 2 * ROUND], BF16, name="h0g", bufs=3, align_bytes=64)
-            if u < 2:
-                bank = transpose_half(x_first[u], 0, False)
-            else:
-                bank = transpose_half(x_sb[u // 2 - 1], u % 2, False)
+            h0g[u] = work.tile([P, 4 * UNIT], BF16, name="h0g", bufs=3, align_bytes=64)
+            bank = transpose_half(x_first[u], 0) if u < 2 else transpose_half(x_sb[u // 2 - 1], u % 2)
             nc.vector.tensor_tensor(
                 out=h0g[u][:].rearrange("p (t u e) -> p t u e", u=2, e=2),
                 in0=bank[:].bitcast(BF16).rearrange("p (u t e) -> p t u e", u=2, e=2),
-                in1=s0_t[:].unsqueeze(1).to_broadcast([P, 256, 2, 2]),
+                in1=s0_t[:].unsqueeze(1).to_broadcast([P, UNIT, 2, 2]),
                 op=ALU.mult,
             )
 
-        def quantise(grouped, width, label):
-            codes = work.tile([P, width], U32, name="c_" + label, bufs=4, align_bytes=64)
-            scales = work.tile([P, width], U8, name="s_" + label, bufs=4, align_bytes=64)
+        def quantise(grouped, label):
+            codes = work.tile([P, UNIT], U32, name="c_" + label, bufs=4, align_bytes=64)
+            scales = work.tile([P, UNIT], U8, name="s_" + label, bufs=4, align_bytes=64)
             nc.vector.quantize_mx(out=codes[:].bitcast(FP8X4), scales=scales[:], in_=grouped[:])
             return codes, scales
 
@@ -157,28 +143,9 @@ def tile_doublebinarylinear_t_kernel(tc, x, scaling0, B, scaling2, A, scaling4, 
             nc.vector.tensor_tensor(
                 out=view[:, il * P : (il + 1) * P, :],
                 in0=bank[:].rearrange("p (j t) -> p t j", j=4),
-                in1=s2_t[:].unsqueeze(1).to_broadcast([P, P, 4]),
+                in1=s2_t[:].rearrange("p u e -> p (u e)").unsqueeze(1).to_broadcast([P, P, 4]),
                 op=ALU.mult,
             )
-
-        def scale_and_bias(eng, u, c, src):
-            if eng == "v":
-                nc.vector.tensor_scalar(
-                    out=y_t[u][:, c, :],
-                    in0=src,
-                    scalar1=s4_t[:, c : c + 1],
-                    scalar2=bias_t[:, c : c + 1],
-                    op0=ALU.mult,
-                    op1=ALU.add,
-                )
-            else:
-                nc.scalar.activation(
-                    out=y_t[u][:, c, :],
-                    in_=src,
-                    func=ACT.Identity,
-                    bias=bias_t[:, c : c + 1],
-                    scale=s4_t[:, c : c + 1],
-                )
 
         def second_matmul(u, pair):
             if pair == 0:
@@ -197,7 +164,25 @@ def tile_doublebinarylinear_t_kernel(tc, x, scaling0, B, scaling2, A, scaling4, 
                     stop=True,
                 )
             for k in range(2):
-                scale_and_bias("v" if u >= UNITS - TAIL_E2 and pair == 1 else "s", u, 2 * pair + k, bank[:, k * UNIT : (k + 1) * UNIT])
+                c = 2 * pair + k
+                src = bank[:, k * UNIT : (k + 1) * UNIT]
+                if u >= UNITS - TAIL_E2 and pair == 1:
+                    nc.vector.tensor_scalar(
+                        out=y_t[u][:, c, :],
+                        in0=src,
+                        scalar1=s4_t[:, c : c + 1],
+                        scalar2=bias_t[:, c : c + 1],
+                        op0=ALU.mult,
+                        op1=ALU.add,
+                    )
+                else:
+                    nc.scalar.activation(
+                        out=y_t[u][:, c, :],
+                        in_=src,
+                        func=ACT.Identity,
+                        bias=bias_t[:, c : c + 1],
+                        scale=s4_t[:, c : c + 1],
+                    )
 
         def finish(u):
             r = u // 2
@@ -212,31 +197,31 @@ def tile_doublebinarylinear_t_kernel(tc, x, scaling0, B, scaling2, A, scaling4, 
                     nc.vector.tensor_copy(out=o_sb[:, il, :], in_=bank[:])
                 else:
                     nc.scalar.copy(out=o_sb[:, il, :], in_=bank[:])
-                if u == UNITS - 1:
+                if u >= UNITS - FINE:
                     nc.sync.dma_start(out=out_rounds[r][:, i : i + 1, :], in_=o_sb[:, il : il + 1, :])
-            if u < UNITS - 1:
+            if u < UNITS - FINE:
                 nc.sync.dma_start(out=out_rounds[r][:, 2 * half : 2 * half + 2, :], in_=o_sb[:])
 
         b_codes, b_scales = None, None
         a_codes, a_scales = None, None
 
-        for s in range(-3, UNITS + FIN):
+        for s in range(-3, UNITS + 3):
+            if unit_ok(s + 2):
+                h0q[s + 2] = quantise(h0g[s + 2], "h0")
             if unit_ok(s + 3):
                 x_unit(s + 3)
             if s == -3:
-                b_codes, b_scales = prepare_weight(b_sb, False, True, "b")
-            if unit_ok(s + 2):
-                h0q[s + 2] = quantise(h0g[s + 2], UNIT, "h0")
-            if unit_ok(s - DQ):
-                h2q[s - DQ] = quantise(h2g[s - DQ], UNIT, "h2")
-            if s == AW:
+                b_codes, b_scales = prepare_weight(b_sb, True, "b")
+            if s == 0:
                 nc.scalar.copy(out=s4_t[:], in_=s4_b[:])
                 nc.scalar.copy(out=bias_t[:], in_=bias_b[:])
-                a_codes, a_scales = prepare_weight(a_sb, True, False, "a")
-            if unit_ok(s - FIN):
-                finish(s - FIN)
+                a_codes, a_scales = prepare_weight(a_sb, False, "a")
+            if unit_ok(s):
+                h2q[s] = quantise(h2g[s], "h2")
+            if unit_ok(s - 3):
+                finish(s - 3)
             for n in range(2):
-                if unit_ok(s - M2):
-                    second_matmul(s - M2, n)
+                if unit_ok(s - 1):
+                    second_matmul(s - 1, n)
                 if unit_ok(s + 1):
                     first_matmul(s + 1, n)

@@ -17,9 +17,9 @@ TOKENS = 4 * 2048
 UNIT = 256
 ROUNDS = TOKENS // (2 * UNIT)
 UNITS = 2 * ROUNDS
-TAIL_EO = 5
-TAIL_E2 = 2
-FINE = 2
+TAIL_EO = 4
+TAIL_E2 = 1
+FINE = 1
 FLOPS = 2 * 2 * TOKENS * DIM * DIM
 
 

@@ -99,34 +99,46 @@ def tile_doublebinarylinear_t_kernel(tc, x, scaling0, B, scaling2, A, scaling4, 
             nc.vector.quantize_mx(out=codes[:].bitcast(FP8X4), scales=scales[:], in_=grouped[:])
             return codes, scales
 
-        h0g = {}
+        mixed = {}
         h0q = {}
-        h2g = {}
         h2q = {}
         y_t = {}
+
+        def mixed_tile(s):
+            if s not in mixed:
+                mixed[s] = work.tile([P, 8 * UNIT], BF16, name="mixed", bufs=4, align_bytes=64)
+            return mixed[s]
 
         def unit_ok(u):
             return 0 <= u < UNITS
 
         def x_unit(u):
-            h0g[u] = work.tile([P, 4 * UNIT], BF16, name="h0g", bufs=3, align_bytes=64)
+            h0 = mixed_tile(u - 2)[:, 0 : 4 * UNIT]
             bank = transpose_half(x_first[u], 0) if u < 2 else transpose_half(x_sb[u // 2 - 1], u % 2)
             nc.vector.tensor_tensor(
-                out=h0g[u][:].rearrange("p (t u e) -> p t u e", u=2, e=2),
+                out=h0.rearrange("p (t u e) -> p t u e", u=2, e=2),
                 in0=bank[:].bitcast(BF16).rearrange("p (u t e) -> p t u e", u=2, e=2),
                 in1=s0_t[:].unsqueeze(1).to_broadcast([P, UNIT, 2, 2]),
                 op=ALU.mult,
             )
 
-        def quantise(grouped, label):
-            codes = work.tile([P, UNIT], U32, name="c_" + label, bufs=4, align_bytes=64)
-            scales = work.tile([P, UNIT], U8, name="s_" + label, bufs=4, align_bytes=64)
-            nc.vector.quantize_mx(out=codes[:].bitcast(FP8X4), scales=scales[:], in_=grouped[:])
-            return codes, scales
+        def quantise_step(s):
+            first = 0 if unit_ok(s + 2) else 1
+            last = 2 if unit_ok(s) else 1
+            if first == last:
+                return
+            codes = work.tile([P, 2 * UNIT], U32, name="codes", bufs=5, align_bytes=64)
+            scales = work.tile([P, 2 * UNIT], U8, name="scales", bufs=5, align_bytes=64)
+            span = slice(first * UNIT, last * UNIT)
+            nc.vector.quantize_mx(
+                out=codes[:, span].bitcast(FP8X4),
+                scales=scales[:, span],
+                in_=mixed_tile(s)[:, 4 * first * UNIT : 4 * last * UNIT],
+            )
+            h0q[s + 2] = codes[:, 0:UNIT], scales[:, 0:UNIT]
+            h2q[s] = codes[:, UNIT : 2 * UNIT], scales[:, UNIT : 2 * UNIT]
 
         def first_matmul(u, il):
-            if il == 0:
-                h2g[u] = work.tile([P, 4 * UNIT], BF16, name="h2g", bufs=4, align_bytes=64)
             codes, scales = h0q[u]
             bank = new_bank()
             for j in range(4):
@@ -139,7 +151,7 @@ def tile_doublebinarylinear_t_kernel(tc, x, scaling0, B, scaling2, A, scaling4, 
                     start=True,
                     stop=True,
                 )
-            view = h2g[u][:].rearrange("p (t j) -> p t j", j=4)
+            view = mixed_tile(u)[:, 4 * UNIT : 8 * UNIT].rearrange("p (t j) -> p t j", j=4)
             nc.vector.tensor_tensor(
                 out=view[:, il * P : (il + 1) * P, :],
                 in0=bank[:].rearrange("p (j t) -> p t j", j=4),
@@ -158,8 +170,8 @@ def tile_doublebinarylinear_t_kernel(tc, x, scaling0, B, scaling2, A, scaling4, 
                     out=bank[:, k * UNIT : (k + 1) * UNIT],
                     lhsT=a_codes[:, c * P : (c + 1) * P].bitcast(FP8X4),
                     lhsT_scale=a_scales[:, c * P : (c + 1) * P],
-                    rhs=codes[:].bitcast(FP8X4),
-                    rhs_scale=scales[:],
+                    rhs=codes.bitcast(FP8X4),
+                    rhs_scale=scales,
                     start=True,
                     stop=True,
                 )
@@ -206,8 +218,8 @@ def tile_doublebinarylinear_t_kernel(tc, x, scaling0, B, scaling2, A, scaling4, 
         a_codes, a_scales = None, None
 
         for s in range(-3, UNITS + 3):
-            if unit_ok(s + 2):
-                h0q[s + 2] = quantise(h0g[s + 2], "h0")
+            if s < 0:
+                quantise_step(s)
             if unit_ok(s + 3):
                 x_unit(s + 3)
             if s == -3:
@@ -216,8 +228,8 @@ def tile_doublebinarylinear_t_kernel(tc, x, scaling0, B, scaling2, A, scaling4, 
                 nc.scalar.copy(out=s4_t[:], in_=s4_b[:])
                 nc.scalar.copy(out=bias_t[:], in_=bias_b[:])
                 a_codes, a_scales = prepare_weight(a_sb, False, "a")
-            if unit_ok(s):
-                h2q[s] = quantise(h2g[s], "h2")
+            if s >= 0:
+                quantise_step(s)
             if unit_ok(s - 3):
                 finish(s - 3)
             for n in range(2):

@@ -18,8 +18,10 @@ UNIT = 256
 ROUNDS = TOKENS // (2 * UNIT)
 UNITS = 2 * ROUNDS
 TAIL_EO = 4
-TAIL_E2 = 1
-FINE = 1
+TAIL_E2 = 2
+FINE = 4
+WARM_FIRST = 6
+WARM_LATER = 2
 FLOPS = 2 * 2 * TOKENS * DIM * DIM
 
 
@@ -68,12 +70,20 @@ def tile_doublebinarylinear_t_kernel(tc, x, scaling0, B, scaling2, A, scaling4, 
         s4_t = keep.tile([P, 4], F32, name="s4_t")
         bias_t = keep.tile([P, 4], F32, name="bias_t")
 
+        zeros = keep.tile([P, DIM], BF16, name="zeros")
+        nc.vector.memset(zeros[:], 0.0)
+
         banks_made = []
 
         def new_bank():
             n = len(banks_made) % 8
             banks_made.append(n)
             return psum.tile([P, 512], F32, name="bank%d" % n, tag="bank%d" % n)
+
+        def keep_clock(n):
+            bank = new_bank()
+            for k in range(n):
+                nc.tensor.matmul(bank[:], lhsT=zeros[:, 0:P], rhs=zeros[:], start=True, stop=True)
 
         def transpose_half(src, half):
             bank = new_bank()
@@ -220,8 +230,12 @@ def tile_doublebinarylinear_t_kernel(tc, x, scaling0, B, scaling2, A, scaling4, 
         for s in range(-3, UNITS + 3):
             if s < 0:
                 quantise_step(s)
+            if s == -3:
+                keep_clock(WARM_FIRST)
             if unit_ok(s + 3):
                 x_unit(s + 3)
+            if s == -2:
+                keep_clock(WARM_LATER)
             if s == -3:
                 b_codes, b_scales = prepare_weight(b_sb, True, "b")
             if s == 0:

@@ -20,7 +20,7 @@ UNITS = 2 * ROUNDS
 TAIL_EO = 4
 TAIL_E2 = 2
 FINE = 4
-WARM_FIRST = 6
+WARM_FIRST = 4
 WARM_LATER = 2
 FLOPS = 2 * 2 * TOKENS * DIM * DIM
 
@@ -94,19 +94,25 @@ def tile_doublebinarylinear_t_kernel(tc, x, scaling0, B, scaling2, A, scaling4, 
                     nc.tensor.transpose(bank[:, col : col + P], words[:, u * P : (u + 1) * P], ident[:])
             return bank
 
-        def prepare_weight(src, share, label):
-            grouped = keep.tile([P, 4 * DIM], BF16, name="g_" + label, align_bytes=64)
-            codes = keep.tile([P, DIM], U32, name="c_" + label, align_bytes=64)
-            scales = keep.tile([P, DIM], U8, name="s_" + label, align_bytes=64)
+        def prepare_weight(src, pieces, label):
+            grouped = keep.tile([P, 4 * DIM], BF16, name="g_" + label, align_bytes=256)
+            codes = keep.tile([P, DIM], U32, name="c_" + label, align_bytes=256)
+            scales = keep.tile([P, DIM], U8, name="s_" + label, align_bytes=256)
             g_words = grouped[:].bitcast(F32).rearrange("p (t u) -> p t u", u=2)
             for half in range(2):
                 bank = transpose_half(src, half)
-                words = bank[:].rearrange("p (u t) -> p t u", u=2)
-                if half == 0 and share:
-                    nc.vector.tensor_copy(out=g_words[:, half * 256 : (half + 1) * 256, :], in_=words)
-                else:
-                    nc.scalar.copy(out=g_words[:, half * 256 : (half + 1) * 256, :], in_=words)
-            nc.vector.quantize_mx(out=codes[:].bitcast(FP8X4), scales=scales[:], in_=grouped[:])
+                nc.scalar.copy(
+                    out=g_words[:, half * UNIT : (half + 1) * UNIT, :],
+                    in_=bank[:].rearrange("p (u t) -> p t u", u=2),
+                )
+            width = DIM // pieces
+            for piece in range(pieces):
+                span = slice(piece * width, (piece + 1) * width)
+                nc.vector.quantize_mx(
+                    out=codes[:, span].bitcast(FP8X4),
+                    scales=scales[:, span],
+                    in_=grouped[:, 4 * piece * width : 4 * (piece + 1) * width],
+                )
             return codes, scales
 
         mixed = {}
@@ -116,7 +122,7 @@ def tile_doublebinarylinear_t_kernel(tc, x, scaling0, B, scaling2, A, scaling4, 
 
         def mixed_tile(s):
             if s not in mixed:
-                mixed[s] = work.tile([P, 8 * UNIT], BF16, name="mixed", bufs=4, align_bytes=64)
+                mixed[s] = work.tile([P, 8 * UNIT], BF16, name="mixed", bufs=4, align_bytes=256)
             return mixed[s]
 
         def unit_ok(u):
@@ -137,8 +143,8 @@ def tile_doublebinarylinear_t_kernel(tc, x, scaling0, B, scaling2, A, scaling4, 
             last = 2 if unit_ok(s) else 1
             if first == last:
                 return
-            codes = work.tile([P, 2 * UNIT], U32, name="codes", bufs=5, align_bytes=64)
-            scales = work.tile([P, 2 * UNIT], U8, name="scales", bufs=5, align_bytes=64)
+            codes = work.tile([P, 2 * UNIT], U32, name="codes", bufs=5, align_bytes=256)
+            scales = work.tile([P, 2 * UNIT], U8, name="scales", bufs=5, align_bytes=256)
             span = slice(first * UNIT, last * UNIT)
             nc.vector.quantize_mx(
                 out=codes[:, span].bitcast(FP8X4),
@@ -237,11 +243,11 @@ def tile_doublebinarylinear_t_kernel(tc, x, scaling0, B, scaling2, A, scaling4, 
             if s == -2:
                 keep_clock(WARM_LATER)
             if s == -3:
-                b_codes, b_scales = prepare_weight(b_sb, True, "b")
+                b_codes, b_scales = prepare_weight(b_sb, 2, "b")
             if s == 0:
                 nc.scalar.copy(out=s4_t[:], in_=s4_b[:])
                 nc.scalar.copy(out=bias_t[:], in_=bias_b[:])
-                a_codes, a_scales = prepare_weight(a_sb, False, "a")
+                a_codes, a_scales = prepare_weight(a_sb, 1, "a")
             if s >= 0:
                 quantise_step(s)
             if unit_ok(s - 3):

from contextlib import ExitStack

import concourse.mybir as mybir
from concourse.masks import make_identity

F32 = mybir.dt.float32
BF16 = mybir.dt.bfloat16
U32 = mybir.dt.uint32
U8 = mybir.dt.uint8
FP8X4 = mybir.dt.float8_e4m3fn_x4
ACT = mybir.ActivationFunctionType
ALU = mybir.AluOpType

P = 128
DIM = 512
TOKENS = 4 * 2048
UNIT = 256
ROUNDS = TOKENS // (2 * UNIT)
UNITS = 2 * ROUNDS
TAIL_EO = 4
TAIL_E2 = 2
FINE = 4
WARM_FIRST = 4
WARM_LATER = 2
FLOPS = 2 * 2 * TOKENS * DIM * DIM


def tile_doublebinarylinear_t_kernel(tc, x, scaling0, B, scaling2, A, scaling4, bias, out):
    nc = tc.nc
    x_rounds = x.flatten_outer_dims().rearrange("(r p i) k -> r p i k", p=P, i=4)
    out_rounds = out.flatten_outer_dims().rearrange("(r p i) o -> r p i o", p=P, i=4)

    with ExitStack() as ctx:
        ctx.enter_context(tc.manual_schedule())
        keep = ctx.enter_context(tc.tile_pool(name="keep", bufs=1))
        work = ctx.enter_context(tc.tile_pool(name="work", bufs=2))
        psum = ctx.enter_context(tc.psum_pool(name="psum", bufs=1))

        s0_t = keep.tile([P, 2, 2], BF16, name="s0_t")
        s2_t = keep.tile([P, 2, 2], BF16, name="s2_t")
        s4_b = keep.tile([P, 4], BF16, name="s4_b")
        bias_b = keep.tile([P, 4], BF16, name="bias_b")
        nc.scalar.dma_start(out=s0_t[:], in_=scaling0.rearrange("(u p e) -> p u e", u=2, e=2))
        nc.scalar.dma_start(out=s2_t[:], in_=scaling2.rearrange("(u q e) -> q u e", u=2, e=2))

        b_sb = keep.tile([P, 4, DIM], BF16, name="b_sb")
        a_sb = keep.tile([P, 4, DIM], BF16, name="a_sb")
        x_first = [keep.tile([P, 2, DIM], BF16, name="x_first%d" % u) for u in range(2)]
        x_sb = [keep.tile([P, 4, DIM], BF16, name="x_sb%d" % r) for r in range(1, ROUNDS)]
        b_view = B.rearrange("(u q e) k -> q u e k", u=2, e=2)
        nc.sync.dma_start(out=x_first[0][:], in_=x_rounds[0][:, 0:2, :])
        for u in range(2):
            nc.sync.dma_start(out=b_sb[:, 2 * u : 2 * u + 2, :], in_=b_view[:, u, :, :])
        nc.sync.dma_start(out=x_first[1][:], in_=x_rounds[0][:, 2:4, :])
        nc.sync.dma_start(out=x_sb[0][:], in_=x_rounds[1])
        nc.sync.dma_start(out=a_sb[:], in_=A.rearrange("(c r) m -> r c m", c=4))
        with nc.allow_non_contiguous_dma(reason="two vectors of 512 values, one value a partition and chunk"):
            nc.sync.dma_start(out=s4_b[:], in_=scaling4.rearrange("(c r) -> r c", c=4))
            nc.sync.dma_start(out=bias_b[:], in_=bias.rearrange("(c r) -> r c", c=4))
        for r in range(2, ROUNDS):
            nc.sync.dma_start(out=x_sb[r - 1][:], in_=x_rounds[r])

        warm_in = keep.tile([P, 1], F32, name="warm_in")
        warm_out = keep.tile([P, 1], F32, name="warm_out")
        nc.vector.memset(warm_in[:], 0.0)
        nc.scalar.copy(out=warm_out[:], in_=warm_in[:])

        ident = keep.tile([P, P], F32, name="ident")
        make_identity(nc, ident[:])
        s4_t = keep.tile([P, 4], F32, name="s4_t")
        bias_t = keep.tile([P, 4], F32, name="bias_t")

        zeros = keep.tile([P, DIM], BF16, name="zeros")
        nc.vector.memset(zeros[:], 0.0)

        banks_made = []

        def new_bank():
            n = len(banks_made) % 8
            banks_made.append(n)
            return psum.tile([P, 512], F32, name="bank%d" % n, tag="bank%d" % n)

        def keep_clock(n):
            bank = new_bank()
            for k in range(n):
                nc.tensor.matmul(bank[:], lhsT=zeros[:, 0:P], rhs=zeros[:], start=True, stop=True)

        def transpose_half(src, half):
            bank = new_bank()
            for u in range(2):
                for il in range(2):
                    words = src[:, 2 * half + il, :].bitcast(F32)
                    col = (2 * u + il) * P
                    nc.tensor.transpose(bank[:, col : col + P], words[:, u * P : (u + 1) * P], ident[:])
            return bank

        def prepare_weight(src, pieces, label):
            grouped = keep.tile([P, 4 * DIM], BF16, name="g_" + label, align_bytes=256)
            codes = keep.tile([P, DIM], U32, name="c_" + label, align_bytes=256)
            scales = keep.tile([P, DIM], U8, name="s_" + label, align_bytes=256)
            g_words = grouped[:].bitcast(F32).rearrange("p (t u) -> p t u", u=2)
            for half in range(2):
                bank = transpose_half(src, half)
                nc.scalar.copy(
                    out=g_words[:, half * UNIT : (half + 1) * UNIT, :],
                    in_=bank[:].rearrange("p (u t) -> p t u", u=2),
                )
            width = DIM // pieces
            for piece in range(pieces):
                span = slice(piece * width, (piece + 1) * width)
                nc.vector.quantize_mx(
                    out=codes[:, span].bitcast(FP8X4),
                    scales=scales[:, span],
                    in_=grouped[:, 4 * piece * width : 4 * (piece + 1) * width],
                )
            return codes, scales

        mixed = {}
        h0q = {}
        h2q = {}
        y_t = {}

        def mixed_tile(s):
            if s not in mixed:
                mixed[s] = work.tile([P, 8 * UNIT], BF16, name="mixed", bufs=4, align_bytes=256)
            return mixed[s]

        def unit_ok(u):
            return 0 <= u < UNITS

        def x_unit(u):
            h0 = mixed_tile(u - 2)[:, 0 : 4 * UNIT]
            bank = transpose_half(x_first[u], 0) if u < 2 else transpose_half(x_sb[u // 2 - 1], u % 2)
            nc.vector.tensor_tensor(
                out=h0.rearrange("p (t u e) -> p t u e", u=2, e=2),
                in0=bank[:].bitcast(BF16).rearrange("p (u t e) -> p t u e", u=2, e=2),
                in1=s0_t[:].unsqueeze(1).to_broadcast([P, UNIT, 2, 2]),
                op=ALU.mult,
            )

        def quantise_step(s):
            first = 0 if unit_ok(s + 2) else 1
            last = 2 if unit_ok(s) else 1
            if first == last:
                return
            codes = work.tile([P, 2 * UNIT], U32, name="codes", bufs=5, align_bytes=256)
            scales = work.tile([P, 2 * UNIT], U8, name="scales", bufs=5, align_bytes=256)
            span = slice(first * UNIT, last * UNIT)
            nc.vector.quantize_mx(
                out=codes[:, span].bitcast(FP8X4),
                scales=scales[:, span],
                in_=mixed_tile(s)[:, 4 * first * UNIT : 4 * last * UNIT],
            )
            h0q[s + 2] = codes[:, 0:UNIT], scales[:, 0:UNIT]
            h2q[s] = codes[:, UNIT : 2 * UNIT], scales[:, UNIT : 2 * UNIT]

        def first_matmul(u, il):
            codes, scales = h0q[u]
            bank = new_bank()
            for j in range(4):
                nc.tensor.matmul_mx(
                    out=bank[:, j * P : (j + 1) * P],
                    lhsT=b_codes[:, j * P : (j + 1) * P].bitcast(FP8X4),
                    lhsT_scale=b_scales[:, j * P : (j + 1) * P],
                    rhs=codes[:, il * P : (il + 1) * P].bitcast(FP8X4),
                    rhs_scale=scales[:, il * P : (il + 1) * P],
                    start=True,
                    stop=True,
                )
            view = mixed_tile(u)[:, 4 * UNIT : 8 * UNIT].rearrange("p (t j) -> p t j", j=4)
            nc.vector.tensor_tensor(
                out=view[:, il * P : (il + 1) * P, :],
                in0=bank[:].rearrange("p (j t) -> p t j", j=4),
                in1=s2_t[:].rearrange("p u e -> p (u e)").unsqueeze(1).to_broadcast([P, P, 4]),
                op=ALU.mult,
            )

        def second_matmul(u, pair):
            if pair == 0:
                y_t[u] = work.tile([P, 4, UNIT], F32, name="y_t", bufs=4)
            codes, scales = h2q[u]
            bank = new_bank()
            for k in range(2):
                c = 2 * pair + k
                nc.tensor.matmul_mx(
                    out=bank[:, k * UNIT : (k + 1) * UNIT],
                    lhsT=a_codes[:, c * P : (c + 1) * P].bitcast(FP8X4),
                    lhsT_scale=a_scales[:, c * P : (c + 1) * P],
                    rhs=codes.bitcast(FP8X4),
                    rhs_scale=scales,
                    start=True,
                    stop=True,
                )
            for k in range(2):
                c = 2 * pair + k
                src = bank[:, k * UNIT : (k + 1) * UNIT]
                if u >= UNITS - TAIL_E2 and pair == 1:
                    nc.vector.tensor_scalar(
                        out=y_t[u][:, c, :],
                        in0=src,
                        scalar1=s4_t[:, c : c + 1],
                        scalar2=bias_t[:, c : c + 1],
                        op0=ALU.mult,
                        op1=ALU.add,
                    )
                else:
                    nc.scalar.activation(
                        out=y_t[u][:, c, :],
                        in_=src,
                        func=ACT.Identity,
                        bias=bias_t[:, c : c + 1],
                        scale=s4_t[:, c : c + 1],
                    )

        def finish(u):
            r = u // 2
            half = u % 2
            o_sb = work.tile([P, 2, DIM], F32, name="o_sb", bufs=6)
            for il in range(2):
                i = 2 * half + il
                bank = new_bank()
                for c in range(4):
                    nc.tensor.transpose(bank[:, c * P : (c + 1) * P], y_t[u][:, c, il * P : (il + 1) * P], ident[:])
                if u >= UNITS - TAIL_EO and il == 1:
                    nc.vector.tensor_copy(out=o_sb[:, il, :], in_=bank[:])
                else:
                    nc.scalar.copy(out=o_sb[:, il, :], in_=bank[:])
                if u >= UNITS - FINE:
                    nc.sync.dma_start(out=out_rounds[r][:, i : i + 1, :], in_=o_sb[:, il : il + 1, :])
            if u < UNITS - FINE:
                nc.sync.dma_start(out=out_rounds[r][:, 2 * half : 2 * half + 2, :], in_=o_sb[:])

        b_codes, b_scales = None, None
        a_codes, a_scales = None, None

        for s in range(-3, UNITS + 3):
            if s < 0:
                quantise_step(s)
            if s == -3:
                keep_clock(WARM_FIRST)
            if unit_ok(s + 3):
                x_unit(s + 3)
            if s == -2:
                keep_clock(WARM_LATER)
            if s == -3:
                b_codes, b_scales = prepare_weight(b_sb, 2, "b")
            if s == 0:
                nc.scalar.copy(out=s4_t[:], in_=s4_b[:])
                nc.scalar.copy(out=bias_t[:], in_=bias_b[:])
                a_codes, a_scales = prepare_weight(a_sb, 1, "a")
            if s >= 0:
                quantise_step(s)
            if unit_ok(s - 3):
                finish(s - 3)
            for n in range(2):
                if unit_ok(s - 1):
                    second_matmul(s - 1, n)
                if unit_ok(s + 1):
                    first_matmul(s + 1, n)
